import numpy as np
import ml_dtypes


def mxq(x, axis, fmt="e4m3"):
    dtype, down = {"e4m3": (ml_dtypes.float8_e4m3fn, 7), "e5m2": (ml_dtypes.float8_e5m2, 14)}[fmt]
    v = np.moveaxis(np.asarray(x, np.float32).astype(ml_dtypes.bfloat16).astype(np.float64), axis, -1)
    blocks = v.reshape(v.shape[:-1] + (-1, 32))
    amax = np.abs(blocks).max(-1, keepdims=True)
    byte = np.maximum(np.where(amax > 0, np.frexp(amax)[1] - 1 + 127, 0) - down, 1)
    scale = np.exp2(byte - 127.0)
    codes = (blocks / scale).astype(np.float32).astype(dtype).astype(np.float64)
    return np.moveaxis((codes * scale).reshape(v.shape), -1, axis)


WIDE = False


def mx_kscale(k):
    if not WIDE:
        return np.ones(k)
    levels = np.array([10, -10, 5, -5, 0])
    if k % 512:
        return np.exp2(np.random.permutation(np.resize(levels, k // 32))).repeat(32)
    a = np.empty((k // 512, 16))
    for p in range(k // 512):
        a[p, :8] = np.random.permutation(np.resize(levels, 8))
        for g in range(8):
            far = levels[np.abs(levels - a[p, g]) >= 10]
            a[p, g + 8] = far[np.random.randint(len(far))]
    return np.exp2(a.ravel()).repeat(32)


BF16 = ml_dtypes.bfloat16


def bf(x):
    return np.asarray(x, np.float32).astype(BF16)


def f64(x):
    return np.asarray(x).astype(np.float64)


B, N, D, C = 2048, 2048, 512, 8

SIGMA = 1.0


def setup_inputs():
    s = mx_kscale(B)
    u = mx_kscale(N)
    centres = (0.8 * np.random.standard_normal((1, D)) + 0.9 * np.random.standard_normal((C, D))) / np.sqrt(D)

    def draw(rows):
        amp = 0.5 + np.random.random((rows, 1))
        return bf(centres[np.random.randint(0, C, rows)] * amp + np.random.standard_normal((rows, D)) * 0.7 / np.sqrt(D))

    x0 = draw(B)
    t0 = draw(N)
    g = bf(np.random.standard_normal((B, N)) * np.exp2(np.random.randint(-6, 1, (B, 1))) * 16.0 / s[:, None] * u[None, :])
    xf, tf = f64(x0), f64(t0)
    dist = np.sum(xf * xf, axis=-1, keepdims=True) + np.sum(tf * tf, axis=-1)[None, :] - 2.0 * (xf @ tf.T)
    return {"inputs": bf(xf * s[:, None] / np.max(u)), "train_data": bf(tf / u[:, None] * np.min(s)),
            "dist": np.asarray(dist, np.float32), "grad_out": g}


def reference(inputs, train_data, dist, grad_out):
    x, t, z = f64(inputs), f64(train_data), f64(dist)
    p = np.where(z > 0.0, np.exp(-np.maximum(z, 0.0) / (2.0 * SIGMA ** 2)), 0.0)
    e = f64(grad_out) * p / SIGMA ** 2
    r = np.sum(e, axis=1, keepdims=True)
    c = np.sum(e, axis=0)[:, None]
    dx = (mxq(e, 1, "e5m2") @ mxq(t, 0, "e4m3")) - x * r
    dt = (mxq(e, 0, "e5m2").T @ mxq(x, 0, "e4m3")) - t * c
    return dx, dt

@@ -1,0 +1,310 @@
+from contextlib import ExitStack
+
+import concourse.mybir as mybir
+from concourse.masks import make_identity
+
+F32 = mybir.dt.float32
+BF16 = mybir.dt.bfloat16
+U32 = mybir.dt.uint32
+U8 = mybir.dt.uint8
+E4 = mybir.dt.float8_e4m3fn_x4
+E5 = mybir.dt.float8_e5m2_x4
+ALU = mybir.AluOpType
+ACT = mybir.ActivationFunctionType
+AX = mybir.AxisListType
+
+B, N, D = 2048, 2048, 512
+P = 128
+PACK = 4
+KP = P * PACK
+G = B // KP
+C = N // KP
+CHUNKS = G * C
+ACC_BANKS = 3
+
+FLOPS = 2 * 2 * B * N * D
+
+
+def tile_patternlayer_t_v_kernel(tc, inputs, train_data, dist, grad_out, out_0, out_1):
+    nc = tc.nc
+    x_v = inputs.rearrange("(g p j) d -> p g j d", p=P, j=PACK)
+    t_v = train_data.rearrange("(g p j) d -> p g j d", p=P, j=PACK)
+    d_v = dist.rearrange("(g p j) n -> p g j n", p=P, j=PACK)
+    g_v = grad_out.rearrange("(g p j) n -> p g j n", p=P, j=PACK)
+    o0_v = out_0.rearrange("(g p j) d -> p g j d", p=P, j=PACK)
+    o1_v = out_1.rearrange("(g p j) d -> p g j d", p=P, j=PACK)
+
+    with ExitStack() as ctx:
+        const = ctx.enter_context(tc.tile_pool(name="const", bufs=1))
+        dpool = ctx.enter_context(tc.tile_pool(name="dpool", bufs=3))
+        ppool = ctx.enter_context(tc.tile_pool(name="ppool", bufs=2))
+        epool = ctx.enter_context(tc.tile_pool(name="epool", bufs=3))
+        qpool = ctx.enter_context(tc.tile_pool(name="qpool", bufs=2))
+        bpool = ctx.enter_context(tc.tile_pool(name="bpool", bufs=2))
+        opool = ctx.enter_context(tc.tile_pool(name="opool", bufs=2))
+        spool = ctx.enter_context(tc.tile_pool(name="spool", bufs=2))
+        psum = ctx.enter_context(tc.psum_pool(name="psum", bufs=1))
+
+        warm = const.tile([P, 1], F32)
+        nc.vector.memset(warm[:], 0.0)
+        nc.scalar.activation(out=warm[:], in_=warm[:], func=ACT.Exp)
+        ident = const.tile([P, P], F32)
+        make_identity(nc, ident[:])
+
+        x_raw = const.tile([P, G, PACK, D], BF16)
+        t_raw = const.tile([P, C, PACK, D], BF16)
+        x_codes = const.tile([P, G, D], U32, align_bytes=64)
+        x_scales = const.tile([P, G, D], U8, align_bytes=64)
+        t_codes = const.tile([P, C, D], U32, align_bytes=64)
+        t_scales = const.tile([P, C, D], U8, align_bytes=64)
+        a_codes = const.tile([P, G, N], U32, align_bytes=64)
+        a_scales = const.tile([P, G, N], U8, align_bytes=64)
+        r_part = const.tile([P, G, PACK, C], F32)
+        c_part = const.tile([P, C, PACK, G], F32)
+
+        ctx.enter_context(tc.manual_schedule())
+
+        d_ts = {}
+        g_ts = {}
+        p_ts = {}
+        e_ts = {}
+        tb_ts = {}
+        cps_ts = {}
+        bin_ts = {}
+        ain_ts = {}
+        bcode_ts = {}
+        bscale_ts = {}
+
+        def load_weight(raw, view, k):
+            nc.sync.dma_start(out=raw[:, k], in_=view[:, k])
+
+        def prep_weight(raw, codes, scales, k):
+            grouped = qpool.tile([P, D, PACK], BF16, align_bytes=64, name="wgrouped", tag="wgrouped")
+            nc.vector.tensor_copy(
+                out=grouped[:].rearrange("p (c i) j -> p c j i", i=PACK),
+                in_=raw[:, k].rearrange("p j (c i) -> p c j i", i=PACK),
+            )
+            nc.vector.quantize_mx(
+                out=codes[:, k, :].bitcast(E4),
+                scales=scales[:, k, :],
+                in_=grouped[:].rearrange("p d j -> p (d j)"),
+            )
+
+        def load(i):
+            g, c = divmod(i, C)
+            cols = slice(c * KP, (c + 1) * KP)
+            d_ts[i] = dpool.tile([P, PACK, KP], F32, name="d_t", tag="d_t")
+            nc.sync.dma_start(out=d_ts[i][:], in_=d_v[:, g, :, cols])
+            g_ts[i] = dpool.tile([P, PACK, KP], BF16, name="g_t", tag="g_t")
+            nc.sync.dma_start(out=g_ts[i][:], in_=g_v[:, g, :, cols])
+
+        def s_exp(i):
+            p_ts[i] = ppool.tile([P, PACK, KP], F32, name="p_t", tag="p_t")
+            nc.scalar.activation(out=p_ts[i][:], in_=d_ts[i][:], func=ACT.Exp, scale=-0.5)
+
+        def v_mask(i, h):
+            rows = slice(2 * h, 2 * h + 2)
+            nc.vector.scalar_tensor_tensor(
+                out=g_ts[i][:, rows],
+                in0=d_ts[i][:, rows],
+                scalar=0.0,
+                in1=g_ts[i][:, rows],
+                op0=ALU.is_gt,
+                op1=ALU.mult,
+            )
+
+        def v_prod(i, j):
+            g, c = divmod(i, C)
+            if j == 0:
+                e_ts[i] = epool.tile([P, PACK, PACK, P], F32, name="e_t", tag="e_t")
+            nc.vector.scalar_tensor_tensor(
+                out=e_ts[i][:, j].rearrange("p t q -> p q t"),
+                in0=p_ts[i][:, j, :].rearrange("p (q t) -> p q t", t=PACK),
+                scalar=1.0,
+                in1=g_ts[i][:, j, :].rearrange("p (q t) -> p q t", t=PACK),
+                op0=ALU.min,
+                op1=ALU.mult,
+                accum_out=r_part[:, g, j, c : c + 1],
+            )
+
+        def pe_tr(i, j):
+            tb = psum.tile([P, PACK, P], F32, name="tb", tag="tb%d" % j)
+            tb_ts[(i, j)] = tb
+            for t in range(PACK):
+                nc.tensor.transpose(tb[:, t, :], e_ts[i][:, j, t, :], ident[:])
+
+        def s_t9(i, j):
+            if j == 0:
+                bin_ts[i] = qpool.tile([P, PACK, P, PACK], BF16, align_bytes=64, name="b_in", tag="b_in")
+            nc.scalar.copy(out=bin_ts[i][:, j], in_=tb_ts[(i, j)][:].rearrange("q t p -> q p t"))
+
+        def pe_csum(i, t):
+            if t == 0:
+                cps_ts[i] = psum.tile([P, PACK, P], F32, name="c_ps", tag="cps")
+            for j in range(PACK):
+                nc.tensor.matmul(
+                    cps_ts[i][:, t, :],
+                    lhsT=e_ts[i][:, j, t, :],
+                    rhs=ident[:],
+                    is_transpose=True,
+                    start=(j == 0),
+                    stop=(j == PACK - 1),
+                )
+
+        def s_creduce(i):
+            g, c = divmod(i, C)
+            junk = spool.tile([P, PACK, P], BF16, name="junk", tag="junk")
+            for t in range(PACK):
+                nc.scalar.activation(
+                    out=junk[:, t, :], in_=cps_ts[i][:, t, :], func=ACT.Identity, accum_out=c_part[:, c, t, g : g + 1]
+                )
+
+        def s_t7(i):
+            ain_ts[i] = qpool.tile([P, KP, PACK], BF16, align_bytes=64, name="a_in", tag="a_in")
+            nc.scalar.copy(
+                out=ain_ts[i][:].rearrange("p (c i) j -> p c j i", i=PACK),
+                in_=e_ts[i][:].rearrange("p j t (c i) -> p (t c) j i", i=PACK),
+            )
+
+        def v_quant_b(i):
+            g, c = divmod(i, C)
+            if c == 0:
+                bcode_ts[g] = bpool.tile([P, C, KP], U32, align_bytes=64, name="b_codes", tag="b_codes")
+                bscale_ts[g] = bpool.tile([P, C, KP], U8, align_bytes=64, name="b_scales", tag="b_scales")
+            nc.vector.quantize_mx(
+                out=bcode_ts[g][:, c, :].bitcast(E5),
+                scales=bscale_ts[g][:, c, :],
+                in_=bin_ts[i][:].rearrange("q j p t -> q (j p t)"),
+            )
+
+        def v_quant_a(i):
+            g, c = divmod(i, C)
+            cols = slice(c * KP, (c + 1) * KP)
+            nc.vector.quantize_mx(
+                out=a_codes[:, g, cols].bitcast(E5),
+                scales=a_scales[:, g, cols],
+                in_=ain_ts[i][:].rearrange("p n j -> p (n j)"),
+            )
+
+        def pe_tile(kind, idx, m, acc):
+            for k in range(PACK):
+                if kind == "B":
+                    m_cols = slice(m * P, (m + 1) * P)
+                    nc.tensor.matmul_mx(
+                        out=acc[:],
+                        lhsT=bcode_ts[idx][:, k, m_cols].bitcast(E5),
+                        lhsT_scale=bscale_ts[idx][:, k, m_cols],
+                        rhs=t_codes[:, k, :].bitcast(E4),
+                        rhs_scale=t_scales[:, k, :],
+                        start=(k == 0),
+                        stop=(k == PACK - 1),
+                    )
+                else:
+                    m_cols = slice(idx * KP + m * P, idx * KP + (m + 1) * P)
+                    nc.tensor.matmul_mx(
+                        out=acc[:],
+                        lhsT=a_codes[:, k, m_cols].bitcast(E5),
+                        lhsT_scale=a_scales[:, k, m_cols],
+                        rhs=x_codes[:, k, :].bitcast(E4),
+                        rhs_scale=x_scales[:, k, :],
+                        start=(k == 0),
+                        stop=(k == PACK - 1),
+                    )
+
+        state = {"neg": None, "stage": None, "by_tile": False}
+
+        def v_finish(kind, idx, m, acc, by_tile):
+            parts, raw, out_view = (r_part, x_raw, o0_v) if kind == "B" else (c_part, t_raw, o1_v)
+            if m == 0:
+                neg = spool.tile([P, PACK], F32, name="neg", tag="neg")
+                nc.vector.tensor_reduce(out=neg[:], in_=parts[:, idx], axis=AX.X, op=ALU.add)
+                nc.vector.tensor_scalar_mul(out=neg[:], in0=neg[:], scalar1=-1.0)
+                state["neg"] = neg
+                state["stage"] = opool.tile([P, PACK, D], F32, name="ostage", tag="ostage")
+                state["by_tile"] = by_tile
+            stage = state["stage"]
+            nc.vector.scalar_tensor_tensor(
+                out=stage[:, m, :],
+                in0=raw[:, idx, m, :],
+                scalar=state["neg"][:, m : m + 1],
+                in1=acc[:],
+                op0=ALU.mult,
+                op1=ALU.add,
+            )
+            if state["by_tile"]:
+                nc.sync.dma_start(out=out_view[:, idx, m, :], in_=stage[:, m, :])
+            elif m == PACK - 1:
+                nc.sync.dma_start(out=out_view[:, idx], in_=stage[:])
+
+        LAST = CHUNKS - 1
+        ROW3 = CHUNKS - C
+
+        def ok(i):
+            return 0 <= i <= LAST
+
+        load(0)
+        load_weight(t_raw, t_v, 0)
+        load(1)
+        load_weight(t_raw, t_v, 1)
+        load(2)
+        load_weight(t_raw, t_v, 2)
+        load_weight(t_raw, t_v, 3)
+
+        todo_mx = []
+        todo_finish = []
+        slot = 0
+        tiles = 0
+        for k in range(-1, CHUNKS + 5):
+            for j in range(PACK):
+                slot += 1
+                if j == 0:
+                    if ok(k - 1):
+                        for jj in range(PACK):
+                            s_t9(k - 1, jj)
+                    if ok(k - 2):
+                        s_creduce(k - 2)
+                    if ok(k + 1):
+                        s_exp(k + 1)
+                    if ok(k - 1):
+                        s_t7(k - 1)
+                if ok(k):
+                    v_prod(k, j)
+                if j == 3 and 0 <= k and k + 3 <= LAST:
+                    load(k + 3)
+                if j == 3 and 0 <= k < G:
+                    load_weight(x_raw, x_v, k)
+                if ok(k):
+                    pe_tr(k, j)
+                if ok(k - 1):
+                    if j >= 1:
+                        pe_csum(k - 1, j - 1)
+                    if j == 3:
+                        pe_csum(k - 1, 3)
+                while len(todo_finish) > 0 and todo_finish[0][0] + 2 <= slot:
+                    item = todo_finish.pop(0)
+                    v_finish(item[1], item[2], item[3], item[4], k > LAST)
+                if j == 0 and ok(k - 2):
+                    v_quant_a(k - 2)
+                    if k - 2 >= ROW3:
+                        for m in range(PACK):
+                            todo_mx.append(("A", k - 2 - ROW3, m))
+                if j == 1 and ok(k + 1):
+                    v_mask(k + 1, 0)
+                if j == 2 and ok(k - 1):
+                    v_quant_b(k - 1)
+                    if (k - 1) % C == C - 1:
+                        for m in range(PACK):
+                            todo_mx.append(("B", (k - 1) // C, m))
+                if j == 3:
+                    if ok(k + 1):
+                        v_mask(k + 1, 1)
+                    if -1 <= k <= 2:
+                        prep_weight(t_raw, t_codes, t_scales, k + 1)
+                    if k in (4, 6, 8, 10):
+                        prep_weight(x_raw, x_codes, x_scales, (k - 4) // 2)
+                if len(todo_mx) > 0:
+                    kind, idx, m = todo_mx.pop(0)
+                    acc = psum.tile([P, D], F32, name="acc", tag="acc%d" % (tiles % ACC_BANKS))
+                    tiles += 1
+                    pe_tile(kind, idx, m, acc)
+                    todo_finish.append((slot, kind, idx, m, acc))

@@ -78,12 +78,15 @@ def tile_patternlayer_t_v_kernel(tc, inputs, train_data, dist, grad_out, out_0, 
         def load_weight(raw, view, k):
             nc.sync.dma_start(out=raw[:, k], in_=view[:, k])
 
-        def prep_weight(raw, codes, scales, k):
+        def group_weight(raw, k):
             grouped = qpool.tile([P, D, PACK], BF16, align_bytes=64, name="wgrouped", tag="wgrouped")
             nc.vector.tensor_copy(
                 out=grouped[:].rearrange("p (c i) j -> p c j i", i=PACK),
                 in_=raw[:, k].rearrange("p j (c i) -> p c j i", i=PACK),
             )
+            return grouped
+
+        def quantize_weight(grouped, codes, scales, k):
             nc.vector.quantize_mx(
                 out=codes[:, k, :].bitcast(E4),
                 scales=scales[:, k, :],
@@ -102,15 +105,9 @@ def tile_patternlayer_t_v_kernel(tc, inputs, train_data, dist, grad_out, out_0, 
             p_ts[i] = ppool.tile([P, PACK, KP], F32, name="p_t", tag="p_t")
             nc.scalar.activation(out=p_ts[i][:], in_=d_ts[i][:], func=ACT.Exp, scale=-0.5)
 
-        def v_mask(i, h):
-            rows = slice(2 * h, 2 * h + 2)
+        def v_mask(i):
             nc.vector.scalar_tensor_tensor(
-                out=g_ts[i][:, rows],
-                in0=d_ts[i][:, rows],
-                scalar=0.0,
-                in1=g_ts[i][:, rows],
-                op0=ALU.is_gt,
-                op1=ALU.mult,
+                out=g_ts[i][:], in0=d_ts[i][:], scalar=0.0, in1=g_ts[i][:], op0=ALU.is_gt, op1=ALU.mult
             )
 
         def v_prod(i, j):
@@ -134,7 +131,7 @@ def tile_patternlayer_t_v_kernel(tc, inputs, train_data, dist, grad_out, out_0, 
                 nc.tensor.transpose(tb[:, t, :], e_ts[i][:, j, t, :], ident[:])
 
         def s_t9(i, j):
-            if j == 0:
+            if j == PACK - 1:
                 bin_ts[i] = qpool.tile([P, PACK, P, PACK], BF16, align_bytes=64, name="b_in", tag="b_in")
             nc.scalar.copy(out=bin_ts[i][:, j], in_=tb_ts[(i, j)][:].rearrange("q t p -> q p t"))
 
@@ -154,9 +151,13 @@ def tile_patternlayer_t_v_kernel(tc, inputs, train_data, dist, grad_out, out_0, 
         def s_creduce(i):
             g, c = divmod(i, C)
             junk = spool.tile([P, PACK, P], BF16, name="junk", tag="junk")
-            for t in range(PACK):
+            for t in reversed(range(PACK)):
                 nc.scalar.activation(
-                    out=junk[:, t, :], in_=cps_ts[i][:, t, :], func=ACT.Identity, accum_out=c_part[:, c, t, g : g + 1]
+                    out=junk[:, t, :],
+                    in_=cps_ts[i][:, t, :],
+                    func=ACT.Identity,
+                    scale=-1.0,
+                    accum_out=c_part[:, c, t, g : g + 1],
                 )
 
         def s_t7(i):
@@ -211,22 +212,30 @@ def tile_patternlayer_t_v_kernel(tc, inputs, train_data, dist, grad_out, out_0, 
                         stop=(k == PACK - 1),
                     )
 
-        state = {"neg": None, "stage": None, "by_tile": False}
+        negs = {}
+        state = {"stage": None, "by_tile": False}
+
+        def v_neg(kind, idx):
+            neg = spool.tile([P, PACK], F32, name="neg", tag="neg", bufs=4)
+            if kind == "B":
+                nc.vector.tensor_reduce(out=neg[:], in_=r_part[:, idx], axis=AX.X, op=ALU.add)
+            else:
+                nc.vector.tensor_reduce(out=neg[:], in_=c_part[:, idx], axis=AX.X, op=ALU.add)
+            negs[(kind, idx)] = neg
+
+        def v_flip(kind, idx):
+            nc.vector.tensor_scalar_mul(out=negs[(kind, idx)][:], in0=negs[(kind, idx)][:], scalar1=-1.0)
 
         def v_finish(kind, idx, m, acc, by_tile):
-            parts, raw, out_view = (r_part, x_raw, o0_v) if kind == "B" else (c_part, t_raw, o1_v)
+            raw, out_view = (x_raw, o0_v) if kind == "B" else (t_raw, o1_v)
             if m == 0:
-                neg = spool.tile([P, PACK], F32, name="neg", tag="neg")
-                nc.vector.tensor_reduce(out=neg[:], in_=parts[:, idx], axis=AX.X, op=ALU.add)
-                nc.vector.tensor_scalar_mul(out=neg[:], in0=neg[:], scalar1=-1.0)
-                state["neg"] = neg
                 state["stage"] = opool.tile([P, PACK, D], F32, name="ostage", tag="ostage")
                 state["by_tile"] = by_tile
             stage = state["stage"]
             nc.vector.scalar_tensor_tensor(
                 out=stage[:, m, :],
                 in0=raw[:, idx, m, :],
-                scalar=state["neg"][:, m : m + 1],
+                scalar=negs[(kind, idx)][:, m : m + 1],
                 in1=acc[:],
                 op0=ALU.mult,
                 op1=ALU.add,
@@ -250,61 +259,68 @@ def tile_patternlayer_t_v_kernel(tc, inputs, train_data, dist, grad_out, out_0, 
         load_weight(t_raw, t_v, 2)
         load_weight(t_raw, t_v, 3)
 
+        weight_steps = {-1: ("t", 0), 0: ("t", 1), 1: ("t", 2), 2: ("t", 3), 4: ("x", 0), 6: ("x", 1), 8: ("x", 2), 10: ("x", 3)}
         todo_mx = []
-        todo_finish = []
-        slot = 0
         tiles = 0
-        for k in range(-1, CHUNKS + 5):
-            for j in range(PACK):
-                slot += 1
-                if j == 0:
-                    if ok(k - 1):
-                        for jj in range(PACK):
-                            s_t9(k - 1, jj)
-                    if ok(k - 2):
-                        s_creduce(k - 2)
-                    if ok(k + 1):
-                        s_exp(k + 1)
-                    if ok(k - 1):
-                        s_t7(k - 1)
-                if ok(k):
+        for k in range(-1, CHUNKS + 7):
+            if ok(k - 1):
+                for jj in reversed(range(PACK)):
+                    s_t9(k - 1, jj)
+            if ok(k - 2):
+                s_creduce(k - 2)
+            if ok(k + 1):
+                s_exp(k + 1)
+            if ok(k - 1):
+                s_t7(k - 1)
+
+            if ok(k - 2):
+                v_quant_a(k - 2)
+            if ok(k):
+                for j in range(PACK):
                     v_prod(k, j)
-                if j == 3 and 0 <= k and k + 3 <= LAST:
-                    load(k + 3)
-                if j == 3 and 0 <= k < G:
-                    load_weight(x_raw, x_v, k)
-                if ok(k):
+            if 0 <= k and k + 3 <= LAST:
+                load(k + 3)
+            if 0 <= k < G:
+                load_weight(x_raw, x_v, k)
+            if ROW3 <= k - 2 <= LAST:
+                v_neg("A", k - 2 - ROW3)
+                for m in range(PACK):
+                    todo_mx.append(("A", k - 2 - ROW3, m))
+
+            run = []
+            while len(todo_mx) > 0 and len(run) < ACC_BANKS:
+                kind, idx, m = todo_mx.pop(0)
+                acc = psum.tile([P, D], F32, name="acc", tag="acc%d" % (tiles % ACC_BANKS))
+                tiles += 1
+                pe_tile(kind, idx, m, acc)
+                run.append((kind, idx, m, acc))
+            for item in run:
+                v_finish(item[0], item[1], item[2], item[3], k > LAST)
+
+            if ok(k - 1):
+                for t in range(PACK):
+                    pe_csum(k - 1, t)
+            if ok(k):
+                for j in range(PACK):
                     pe_tr(k, j)
-                if ok(k - 1):
-                    if j >= 1:
-                        pe_csum(k - 1, j - 1)
-                    if j == 3:
-                        pe_csum(k - 1, 3)
-                while len(todo_finish) > 0 and todo_finish[0][0] + 2 <= slot:
-                    item = todo_finish.pop(0)
-                    v_finish(item[1], item[2], item[3], item[4], k > LAST)
-                if j == 0 and ok(k - 2):
-                    v_quant_a(k - 2)
-                    if k - 2 >= ROW3:
-                        for m in range(PACK):
-                            todo_mx.append(("A", k - 2 - ROW3, m))
-                if j == 1 and ok(k + 1):
-                    v_mask(k + 1, 0)
-                if j == 2 and ok(k - 1):
-                    v_quant_b(k - 1)
-                    if (k - 1) % C == C - 1:
-                        for m in range(PACK):
-                            todo_mx.append(("B", (k - 1) // C, m))
-                if j == 3:
-                    if ok(k + 1):
-                        v_mask(k + 1, 1)
-                    if -1 <= k <= 2:
-                        prep_weight(t_raw, t_codes, t_scales, k + 1)
-                    if k in (4, 6, 8, 10):
-                        prep_weight(x_raw, x_codes, x_scales, (k - 4) // 2)
-                if len(todo_mx) > 0:
-                    kind, idx, m = todo_mx.pop(0)
-                    acc = psum.tile([P, D], F32, name="acc", tag="acc%d" % (tiles % ACC_BANKS))
-                    tiles += 1
-                    pe_tile(kind, idx, m, acc)
-                    todo_finish.append((slot, kind, idx, m, acc))
+
+            if ok(k + 1):
+                v_mask(k + 1)
+            grouped = None
+            if k in weight_steps:
+                which, wk = weight_steps[k]
+                grouped = group_weight(t_raw if which == "t" else x_raw, wk)
+            if ok(k - 1):
+                v_quant_b(k - 1)
+                if (k - 1) % C == C - 1:
+                    v_neg("B", (k - 1) // C)
+                    for m in range(PACK):
+                        todo_mx.append(("B", (k - 1) // C, m))
+            if k in weight_steps:
+                which, wk = weight_steps[k]
+                if which == "t":
+                    quantize_weight(grouped, t_codes, t_scales, wk)
+                else:
+                    quantize_weight(grouped, x_codes, x_scales, wk)
+            if ok(k - 1) and (k - 1) % C == C - 1:
+                v_flip("B", (k - 1) // C)

@@ -93,22 +93,35 @@ def tile_patternlayer_t_v_kernel(tc, inputs, train_data, dist, grad_out, out_0, 
                 in_=grouped[:].rearrange("p d j -> p (d j)"),
             )
 
+        def parts(i):
+            if i == 0:
+                return [slice(0, 2), slice(2, PACK)]
+            return [slice(0, PACK)]
+
         def load(i):
             g, c = divmod(i, C)
             cols = slice(c * KP, (c + 1) * KP)
             d_ts[i] = dpool.tile([P, PACK, KP], F32, name="d_t", tag="d_t")
-            nc.sync.dma_start(out=d_ts[i][:], in_=d_v[:, g, :, cols])
             g_ts[i] = dpool.tile([P, PACK, KP], BF16, name="g_t", tag="g_t")
-            nc.sync.dma_start(out=g_ts[i][:], in_=g_v[:, g, :, cols])
+            for rows in parts(i):
+                nc.sync.dma_start(out=d_ts[i][:, rows], in_=d_v[:, g, rows, cols])
+                nc.sync.dma_start(out=g_ts[i][:, rows], in_=g_v[:, g, rows, cols])
 
         def s_exp(i):
             p_ts[i] = ppool.tile([P, PACK, KP], F32, name="p_t", tag="p_t")
-            nc.scalar.activation(out=p_ts[i][:], in_=d_ts[i][:], func=ACT.Exp, scale=-0.5)
+            for rows in parts(i):
+                nc.scalar.activation(out=p_ts[i][:, rows], in_=d_ts[i][:, rows], func=ACT.Exp, scale=-0.5)
 
         def v_mask(i):
-            nc.vector.scalar_tensor_tensor(
-                out=g_ts[i][:], in0=d_ts[i][:], scalar=0.0, in1=g_ts[i][:], op0=ALU.is_gt, op1=ALU.mult
-            )
+            for rows in parts(i):
+                nc.vector.scalar_tensor_tensor(
+                    out=g_ts[i][:, rows],
+                    in0=d_ts[i][:, rows],
+                    scalar=0.0,
+                    in1=g_ts[i][:, rows],
+                    op0=ALU.is_gt,
+                    op1=ALU.mult,
+                )
 
         def v_prod(i, j):
             g, c = divmod(i, C)
@@ -229,6 +242,8 @@ def tile_patternlayer_t_v_kernel(tc, inputs, train_data, dist, grad_out, out_0, 
         def v_finish(kind, idx, m, acc, by_tile):
             raw, out_view = (x_raw, o0_v) if kind == "B" else (t_raw, o1_v)
             if m == 0:
+                if kind == "A":
+                    v_neg(kind, idx)
                 state["stage"] = opool.tile([P, PACK, D], F32, name="ostage", tag="ostage")
                 state["by_tile"] = by_tile
             stage = state["stage"]
@@ -283,7 +298,6 @@ def tile_patternlayer_t_v_kernel(tc, inputs, train_data, dist, grad_out, out_0, 
             if 0 <= k < G:
                 load_weight(x_raw, x_v, k)
             if ROW3 <= k - 2 <= LAST:
-                v_neg("A", k - 2 - ROW3)
                 for m in range(PACK):
                     todo_mx.append(("A", k - 2 - ROW3, m))
 

@@ -144,7 +144,7 @@ def tile_patternlayer_t_v_kernel(tc, inputs, train_data, dist, grad_out, out_0, 
                 nc.tensor.transpose(tb[:, t, :], e_ts[i][:, j, t, :], ident[:])
 
         def s_t9(i, j):
-            if j == PACK - 1:
+            if j == 0:
                 bin_ts[i] = qpool.tile([P, PACK, P, PACK], BF16, align_bytes=64, name="b_in", tag="b_in")
             nc.scalar.copy(out=bin_ts[i][:, j], in_=tb_ts[(i, j)][:].rearrange("q t p -> q p t"))
 
@@ -279,7 +279,7 @@ def tile_patternlayer_t_v_kernel(tc, inputs, train_data, dist, grad_out, out_0, 
         tiles = 0
         for k in range(-1, CHUNKS + 7):
             if ok(k - 1):
-                for jj in reversed(range(PACK)):
+                for jj in range(PACK):
                     s_t9(k - 1, jj)
             if ok(k - 2):
                 s_creduce(k - 2)

from contextlib import ExitStack

import concourse.mybir as mybir
from concourse.masks import make_identity

F32 = mybir.dt.float32
BF16 = mybir.dt.bfloat16
U32 = mybir.dt.uint32
U8 = mybir.dt.uint8
E4 = mybir.dt.float8_e4m3fn_x4
E5 = mybir.dt.float8_e5m2_x4
ALU = mybir.AluOpType
ACT = mybir.ActivationFunctionType
AX = mybir.AxisListType

B, N, D = 2048, 2048, 512
P = 128
PACK = 4
KP = P * PACK
G = B // KP
C = N // KP
CHUNKS = G * C
ACC_BANKS = 3

FLOPS = 2 * 2 * B * N * D


def tile_patternlayer_t_v_kernel(tc, inputs, train_data, dist, grad_out, out_0, out_1):
    nc = tc.nc
    x_v = inputs.rearrange("(g p j) d -> p g j d", p=P, j=PACK)
    t_v = train_data.rearrange("(g p j) d -> p g j d", p=P, j=PACK)
    d_v = dist.rearrange("(g p j) n -> p g j n", p=P, j=PACK)
    g_v = grad_out.rearrange("(g p j) n -> p g j n", p=P, j=PACK)
    o0_v = out_0.rearrange("(g p j) d -> p g j d", p=P, j=PACK)
    o1_v = out_1.rearrange("(g p j) d -> p g j d", p=P, j=PACK)

    with ExitStack() as ctx:
        const = ctx.enter_context(tc.tile_pool(name="const", bufs=1))
        dpool = ctx.enter_context(tc.tile_pool(name="dpool", bufs=3))
        ppool = ctx.enter_context(tc.tile_pool(name="ppool", bufs=2))
        epool = ctx.enter_context(tc.tile_pool(name="epool", bufs=3))
        qpool = ctx.enter_context(tc.tile_pool(name="qpool", bufs=2))
        bpool = ctx.enter_context(tc.tile_pool(name="bpool", bufs=2))
        opool = ctx.enter_context(tc.tile_pool(name="opool", bufs=2))
        spool = ctx.enter_context(tc.tile_pool(name="spool", bufs=2))
        psum = ctx.enter_context(tc.psum_pool(name="psum", bufs=1))

        warm = const.tile([P, 1], F32)
        nc.vector.memset(warm[:], 0.0)
        nc.scalar.activation(out=warm[:], in_=warm[:], func=ACT.Exp)
        ident = const.tile([P, P], F32)
        make_identity(nc, ident[:])

        x_raw = const.tile([P, G, PACK, D], BF16)
        t_raw = const.tile([P, C, PACK, D], BF16)
        x_codes = const.tile([P, G, D], U32, align_bytes=64)
        x_scales = const.tile([P, G, D], U8, align_bytes=64)
        t_codes = const.tile([P, C, D], U32, align_bytes=64)
        t_scales = const.tile([P, C, D], U8, align_bytes=64)
        a_codes = const.tile([P, G, N], U32, align_bytes=64)
        a_scales = const.tile([P, G, N], U8, align_bytes=64)
        r_part = const.tile([P, G, PACK, C], F32)
        c_part = const.tile([P, C, PACK, G], F32)

        ctx.enter_context(tc.manual_schedule())

        d_ts = {}
        g_ts = {}
        p_ts = {}
        e_ts = {}
        tb_ts = {}
        cps_ts = {}
        bin_ts = {}
        ain_ts = {}
        bcode_ts = {}
        bscale_ts = {}

        def load_weight(raw, view, k):
            nc.sync.dma_start(out=raw[:, k], in_=view[:, k])

        def group_weight(raw, k):
            grouped = qpool.tile([P, D, PACK], BF16, align_bytes=64, name="wgrouped", tag="wgrouped")
            nc.vector.tensor_copy(
                out=grouped[:].rearrange("p (c i) j -> p c j i", i=PACK),
                in_=raw[:, k].rearrange("p j (c i) -> p c j i", i=PACK),
            )
            return grouped

        def quantize_weight(grouped, codes, scales, k):
            nc.vector.quantize_mx(
                out=codes[:, k, :].bitcast(E4),
                scales=scales[:, k, :],
                in_=grouped[:].rearrange("p d j -> p (d j)"),
            )

        def parts(i):
            if i == 0:
                return [slice(0, 2), slice(2, PACK)]
            return [slice(0, PACK)]

        def load(i):
            g, c = divmod(i, C)
            cols = slice(c * KP, (c + 1) * KP)
            d_ts[i] = dpool.tile([P, PACK, KP], F32, name="d_t", tag="d_t")
            g_ts[i] = dpool.tile([P, PACK, KP], BF16, name="g_t", tag="g_t")
            for rows in parts(i):
                nc.sync.dma_start(out=d_ts[i][:, rows], in_=d_v[:, g, rows, cols])
                nc.sync.dma_start(out=g_ts[i][:, rows], in_=g_v[:, g, rows, cols])

        def s_exp(i):
            p_ts[i] = ppool.tile([P, PACK, KP], F32, name="p_t", tag="p_t")
            for rows in parts(i):
                nc.scalar.activation(out=p_ts[i][:, rows], in_=d_ts[i][:, rows], func=ACT.Exp, scale=-0.5)

        def v_mask(i):
            for rows in parts(i):
                nc.vector.scalar_tensor_tensor(
                    out=g_ts[i][:, rows],
                    in0=d_ts[i][:, rows],
                    scalar=0.0,
                    in1=g_ts[i][:, rows],
                    op0=ALU.is_gt,
                    op1=ALU.mult,
                )

        def v_prod(i, j):
            g, c = divmod(i, C)
            if j == 0:
                e_ts[i] = epool.tile([P, PACK, PACK, P], F32, name="e_t", tag="e_t")
            nc.vector.scalar_tensor_tensor(
                out=e_ts[i][:, j].rearrange("p t q -> p q t"),
                in0=p_ts[i][:, j, :].rearrange("p (q t) -> p q t", t=PACK),
                scalar=1.0,
                in1=g_ts[i][:, j, :].rearrange("p (q t) -> p q t", t=PACK),
                op0=ALU.min,
                op1=ALU.mult,
                accum_out=r_part[:, g, j, c : c + 1],
            )

        def pe_tr(i, j):
            tb = psum.tile([P, PACK, P], F32, name="tb", tag="tb%d" % j)
            tb_ts[(i, j)] = tb
            for t in range(PACK):
                nc.tensor.transpose(tb[:, t, :], e_ts[i][:, j, t, :], ident[:])

        def s_t9(i, j):
            if j == 0:
                bin_ts[i] = qpool.tile([P, PACK, P, PACK], BF16, align_bytes=64, name="b_in", tag="b_in")
            nc.scalar.copy(out=bin_ts[i][:, j], in_=tb_ts[(i, j)][:].rearrange("q t p -> q p t"))

        def pe_csum(i, t):
            if t == 0:
                cps_ts[i] = psum.tile([P, PACK, P], F32, name="c_ps", tag="cps")
            for j in range(PACK):
                nc.tensor.matmul(
                    cps_ts[i][:, t, :],
                    lhsT=e_ts[i][:, j, t, :],
                    rhs=ident[:],
                    is_transpose=True,
                    start=(j == 0),
                    stop=(j == PACK - 1),
                )

        def s_creduce(i):
            g, c = divmod(i, C)
            junk = spool.tile([P, PACK, P], BF16, name="junk", tag="junk")
            for t in reversed(range(PACK)):
                nc.scalar.activation(
                    out=junk[:, t, :],
                    in_=cps_ts[i][:, t, :],
                    func=ACT.Identity,
                    scale=-1.0,
                    accum_out=c_part[:, c, t, g : g + 1],
                )

        def s_t7(i):
            ain_ts[i] = qpool.tile([P, KP, PACK], BF16, align_bytes=64, name="a_in", tag="a_in")
            nc.scalar.copy(
                out=ain_ts[i][:].rearrange("p (c i) j -> p c j i", i=PACK),
                in_=e_ts[i][:].rearrange("p j t (c i) -> p (t c) j i", i=PACK),
            )

        def v_quant_b(i):
            g, c = divmod(i, C)
            if c == 0:
                bcode_ts[g] = bpool.tile([P, C, KP], U32, align_bytes=64, name="b_codes", tag="b_codes")
                bscale_ts[g] = bpool.tile([P, C, KP], U8, align_bytes=64, name="b_scales", tag="b_scales")
            nc.vector.quantize_mx(
                out=bcode_ts[g][:, c, :].bitcast(E5),
                scales=bscale_ts[g][:, c, :],
                in_=bin_ts[i][:].rearrange("q j p t -> q (j p t)"),
            )

        def v_quant_a(i):
            g, c = divmod(i, C)
            cols = slice(c * KP, (c + 1) * KP)
            nc.vector.quantize_mx(
                out=a_codes[:, g, cols].bitcast(E5),
                scales=a_scales[:, g, cols],
                in_=ain_ts[i][:].rearrange("p n j -> p (n j)"),
            )

        def pe_tile(kind, idx, m, acc):
            for k in range(PACK):
                if kind == "B":
                    m_cols = slice(m * P, (m + 1) * P)
                    nc.tensor.matmul_mx(
                        out=acc[:],
                        lhsT=bcode_ts[idx][:, k, m_cols].bitcast(E5),
                        lhsT_scale=bscale_ts[idx][:, k, m_cols],
                        rhs=t_codes[:, k, :].bitcast(E4),
                        rhs_scale=t_scales[:, k, :],
                        start=(k == 0),
                        stop=(k == PACK - 1),
                    )
                else:
                    m_cols = slice(idx * KP + m * P, idx * KP + (m + 1) * P)
                    nc.tensor.matmul_mx(
                        out=acc[:],
                        lhsT=a_codes[:, k, m_cols].bitcast(E5),
                        lhsT_scale=a_scales[:, k, m_cols],
                        rhs=x_codes[:, k, :].bitcast(E4),
                        rhs_scale=x_scales[:, k, :],
                        start=(k == 0),
                        stop=(k == PACK - 1),
                    )

        negs = {}
        state = {"stage": None, "by_tile": False}

        def v_neg(kind, idx):
            neg = spool.tile([P, PACK], F32, name="neg", tag="neg", bufs=4)
            if kind == "B":
                nc.vector.tensor_reduce(out=neg[:], in_=r_part[:, idx], axis=AX.X, op=ALU.add)
            else:
                nc.vector.tensor_reduce(out=neg[:], in_=c_part[:, idx], axis=AX.X, op=ALU.add)
            negs[(kind, idx)] = neg

        def v_flip(kind, idx):
            nc.vector.tensor_scalar_mul(out=negs[(kind, idx)][:], in0=negs[(kind, idx)][:], scalar1=-1.0)

        def v_finish(kind, idx, m, acc, by_tile):
            raw, out_view = (x_raw, o0_v) if kind == "B" else (t_raw, o1_v)
            if m == 0:
                if kind == "A":
                    v_neg(kind, idx)
                state["stage"] = opool.tile([P, PACK, D], F32, name="ostage", tag="ostage")
                state["by_tile"] = by_tile
            stage = state["stage"]
            nc.vector.scalar_tensor_tensor(
                out=stage[:, m, :],
                in0=raw[:, idx, m, :],
                scalar=negs[(kind, idx)][:, m : m + 1],
                in1=acc[:],
                op0=ALU.mult,
                op1=ALU.add,
            )
            if state["by_tile"]:
                nc.sync.dma_start(out=out_view[:, idx, m, :], in_=stage[:, m, :])
            elif m == PACK - 1:
                nc.sync.dma_start(out=out_view[:, idx], in_=stage[:])

        LAST = CHUNKS - 1
        ROW3 = CHUNKS - C

        def ok(i):
            return 0 <= i <= LAST

        load(0)
        load_weight(t_raw, t_v, 0)
        load(1)
        load_weight(t_raw, t_v, 1)
        load(2)
        load_weight(t_raw, t_v, 2)
        load_weight(t_raw, t_v, 3)

        weight_steps = {-1: ("t", 0), 0: ("t", 1), 1: ("t", 2), 2: ("t", 3), 4: ("x", 0), 6: ("x", 1), 8: ("x", 2), 10: ("x", 3)}
        todo_mx = []
        tiles = 0
        for k in range(-1, CHUNKS + 7):
            if ok(k - 1):
                for jj in range(PACK):
                    s_t9(k - 1, jj)
            if ok(k - 2):
                s_creduce(k - 2)
            if ok(k + 1):
                s_exp(k + 1)
            if ok(k - 1):
                s_t7(k - 1)

            if ok(k - 2):
                v_quant_a(k - 2)
            if ok(k):
                for j in range(PACK):
                    v_prod(k, j)
            if 0 <= k and k + 3 <= LAST:
                load(k + 3)
            if 0 <= k < G:
                load_weight(x_raw, x_v, k)
            if ROW3 <= k - 2 <= LAST:
                for m in range(PACK):
                    todo_mx.append(("A", k - 2 - ROW3, m))

            run = []
            while len(todo_mx) > 0 and len(run) < ACC_BANKS:
                kind, idx, m = todo_mx.pop(0)
                acc = psum.tile([P, D], F32, name="acc", tag="acc%d" % (tiles % ACC_BANKS))
                tiles += 1
                pe_tile(kind, idx, m, acc)
                run.append((kind, idx, m, acc))
            for item in run:
                v_finish(item[0], item[1], item[2], item[3], k > LAST)

            if ok(k - 1):
                for t in range(PACK):
                    pe_csum(k - 1, t)
            if ok(k):
                for j in range(PACK):
                    pe_tr(k, j)

            if ok(k + 1):
                v_mask(k + 1)
            grouped = None
            if k in weight_steps:
                which, wk = weight_steps[k]
                grouped = group_weight(t_raw if which == "t" else x_raw, wk)
            if ok(k - 1):
                v_quant_b(k - 1)
                if (k - 1) % C == C - 1:
                    v_neg("B", (k - 1) // C)
                    for m in range(PACK):
                        todo_mx.append(("B", (k - 1) // C, m))
            if k in weight_steps:
                which, wk = weight_steps[k]
                if which == "t":
                    quantize_weight(grouped, t_codes, t_scales, wk)
                else:
                    quantize_weight(grouped, x_codes, x_scales, wk)
            if ok(k - 1) and (k - 1) % C == C - 1:
                v_flip("B", (k - 1) // C)
